import numpy as np
import ml_dtypes


def mxq(x, axis, fmt="e4m3"):
    dtype, down = {"e4m3": (ml_dtypes.float8_e4m3fn, 7), "e5m2": (ml_dtypes.float8_e5m2, 14)}[fmt]
    v = np.moveaxis(np.asarray(x, np.float32).astype(ml_dtypes.bfloat16).astype(np.float64), axis, -1)
    blocks = v.reshape(v.shape[:-1] + (-1, 32))
    amax = np.abs(blocks).max(-1, keepdims=True)
    byte = np.maximum(np.where(amax > 0, np.frexp(amax)[1] - 1 + 127, 0) - down, 1)
    scale = np.exp2(byte - 127.0)
    codes = (blocks / scale).astype(np.float32).astype(dtype).astype(np.float64)
    return np.moveaxis((codes * scale).reshape(v.shape), -1, axis)


WIDE = False


def mx_kscale(k):
    if not WIDE:
        return np.ones(k)
    levels = np.array([20, -20, 10, -10, 0])
    a = np.random.permutation(np.resize(levels, k // 512 * 4)).reshape(k // 512, 4)
    idx = np.arange(k)
    return np.exp2(a[idx // 512, idx % 128 // 32])


BF16 = ml_dtypes.bfloat16


def bf(x):
    return np.asarray(x, np.float32).astype(BF16)


def f64(x):
    return np.asarray(x).astype(np.float64)


N, CI, CO, H, W, KH, KW = 2, 512, 512, 10, 9, 3, 2
HO, WO = H - KH + 1, W - KW + 1
L = N * HO * WO


def setup_inputs():
    s = mx_kscale(CO)
    x = np.random.standard_normal((N, CI, H, W))
    y = np.random.standard_normal((N, CO, HO, WO)) / np.sqrt(L) / s[None, :, None, None]
    g = np.random.standard_normal((CO, CI, KH, KW)) * np.exp2(np.random.randint(-12, 1, (1, CI, 1, 1))) * s[:, None, None, None]
    return {"input": bf(x), "grad_output": bf(y), "grad_out": bf(g)}


def reference(input, grad_output, grad_out):
    yq = mxq(f64(grad_output).transpose(1, 0, 2, 3).reshape(CO, L), 0, "e4m3")
    gq = mxq(f64(grad_out).reshape(CO, CI * KH * KW), 0, "e5m2").reshape(CO, CI, KH, KW)
    gx = np.zeros((N, CI, H, W))
    for i in range(KH):
        for j in range(KW):
            t = gq[:, :, i, j].T @ yq
            gx[:, :, i:i + HO, j:j + WO] += t.reshape(CI, N, HO, WO).transpose(1, 0, 2, 3)
    return gx

@@ -1,0 +1,106 @@
+from contextlib import ExitStack
+
+import concourse.mybir as mybir
+
+BF16 = mybir.dt.bfloat16
+F32 = mybir.dt.float32
+I32 = mybir.dt.int32
+U32 = mybir.dt.uint32
+U8 = mybir.dt.uint8
+E4M3_X4 = mybir.dt.float8_e4m3fn_x4
+E5M2_X4 = mybir.dt.float8_e5m2_x4
+
+P = 128
+PACK = 4
+IMAGES, CI, CO = 2, 512, 512
+H, W = 10, 9
+KH, KW = 3, 2
+HO, WO = H - KH + 1, W - KW + 1
+TAPS = KH * KW
+CI_TILES = CI // P
+OUT_COLS = IMAGES * H * W
+N_PASS = 512
+TAP_PITCH = 192
+Y_FILLED = TAPS * TAP_PITCH
+Y_COLS = (TAPS - 1) * TAP_PITCH + N_PASS
+VECTOR_TAPS = 3
+
+FLOPS = 2 * CO * CI * TAPS * IMAGES * HO * WO
+BYTES = 2 * IMAGES * CO * HO * WO + 2 * CO * CI * TAPS + 4 * IMAGES * CI * H * W
+
+
+def tile_model_pa_s_kernel(tc, image, grad_output, grad_out, out):
+    nc = tc.nc
+    with ExitStack() as ctx:
+        keep = ctx.enter_context(tc.tile_pool(name="keep", bufs=1))
+        psum = ctx.enter_context(tc.psum_pool(name="psum", bufs=1))
+
+        y_raw = keep.tile([P, IMAGES, PACK, HO * WO], BF16)
+        nc.sync.dma_start(out=y_raw[:], in_=grad_output.rearrange("n (p t) i j -> p n t (i j)", t=PACK))
+        g_rows = grad_out.rearrange("(p t) c kh kw -> p t c (kh kw)", t=PACK)
+        g_raw = []
+        for m in range(CI_TILES):
+            g_raw.append(keep.tile([P, PACK, P, TAPS], BF16, name="g_raw%d" % m))
+            nc.sync.dma_start(out=g_raw[m][:], in_=g_rows[:, :, m * P : (m + 1) * P, :])
+
+        y_shift = keep.tile([P, TAPS, TAP_PITCH, PACK], BF16, align_bytes=64)
+        nc.vector.memset(y_shift[:], 0.0)
+        y_codes = keep.tile([P, Y_COLS], U32, align_bytes=64)
+        y_scales = keep.tile([P, Y_COLS], U8, align_bytes=64)
+        nc.vector.memset(y_codes[:, Y_FILLED:].bitcast(I32), 0)
+        nc.vector.memset(y_scales[:, Y_FILLED:].bitcast(I32), 0)
+
+        y_grouped = keep.tile([P, IMAGES, HO * WO, PACK], BF16)
+        nc.vector.tensor_copy(out=y_grouped[:], in_=y_raw[:].rearrange("p n t l -> p n l t"))
+        y_lines = y_grouped[:].rearrange("p n (i j) t -> p n i (j t)", i=HO)
+        for kh in range(KH):
+            for kw in range(KW):
+                grid = y_shift[:, kh * KW + kw, 0:OUT_COLS, :].rearrange(
+                    "p (n r q) t -> p n r (q t)", n=IMAGES, r=H
+                )
+                nc.vector.tensor_copy(
+                    out=grid[:, :, kh : kh + HO, kw * PACK : (kw + WO) * PACK], in_=y_lines
+                )
+        y_flat = y_shift[:].rearrange("p a c t -> p (a c t)")
+        for first, last in ((0, 1024), (1024, Y_FILLED)):
+            nc.vector.quantize_mx(
+                out=y_codes[:, first:last].bitcast(E4M3_X4),
+                scales=y_scales[:, first:last],
+                in_=y_flat[:, first * PACK : last * PACK],
+            )
+
+        out_rows = out.rearrange("n c r q -> c n (r q)")
+        for m in range(CI_TILES):
+            g_grouped = keep.tile([P, TAPS, P, PACK], BF16, align_bytes=64, name="g_grouped%d" % m)
+            g_taps = g_raw[m][:].rearrange("p t c a -> p a c t")
+            nc.vector.tensor_copy(out=g_grouped[:, :VECTOR_TAPS], in_=g_taps[:, :VECTOR_TAPS])
+            nc.scalar.copy(out=g_grouped[:, VECTOR_TAPS:], in_=g_taps[:, VECTOR_TAPS:])
+
+            g_codes = keep.tile([P, TAPS, P], U32, align_bytes=64, name="g_codes%d" % m)
+            g_scales = keep.tile([P, TAPS, P], U8, align_bytes=64, name="g_scales%d" % m)
+            for kh in range(KH):
+                pair = slice(kh * KW, (kh + 1) * KW)
+                nc.vector.quantize_mx(
+                    out=g_codes[:, pair, :].rearrange("p a c -> p (a c)").bitcast(E5M2_X4),
+                    scales=g_scales[:, pair, :].rearrange("p a c -> p (a c)"),
+                    in_=g_grouped[:, pair].rearrange("p a c t -> p (a c t)"),
+                )
+
+            acc = psum.tile([P, N_PASS], F32, name="acc%d" % m)
+            for tap in range(TAPS):
+                window = slice(tap * TAP_PITCH, tap * TAP_PITCH + N_PASS)
+                nc.tensor.matmul_mx(
+                    out=acc[:],
+                    lhsT=g_codes[:, tap, :].bitcast(E5M2_X4),
+                    lhsT_scale=g_scales[:, tap, :],
+                    rhs=y_codes[:, window].bitcast(E4M3_X4),
+                    rhs_scale=y_scales[:, window],
+                    start=(tap == 0),
+                    stop=(tap == TAPS - 1),
+                )
+            result = keep.tile([P, OUT_COLS], F32, name="result%d" % m)
+            nc.scalar.copy(out=result[:], in_=acc[:, 0:OUT_COLS])
+            nc.sync.dma_start(
+                out=out_rows[m * P : (m + 1) * P],
+                in_=result[:].rearrange("p (n g) -> p n g", n=IMAGES),
+            )

@@ -72,9 +72,10 @@ def tile_model_pa_s_kernel(tc, image, grad_output, grad_out, out):
         out_rows = out.rearrange("n c r q -> c n (r q)")
         for m in range(CI_TILES):
             g_grouped = keep.tile([P, TAPS, P, PACK], BF16, align_bytes=64, name="g_grouped%d" % m)
-            g_taps = g_raw[m][:].rearrange("p t c a -> p a c t")
-            nc.vector.tensor_copy(out=g_grouped[:, :VECTOR_TAPS], in_=g_taps[:, :VECTOR_TAPS])
-            nc.scalar.copy(out=g_grouped[:, VECTOR_TAPS:], in_=g_taps[:, VECTOR_TAPS:])
+            g_from = g_raw[m][:].rearrange("p t c a -> p c a t")
+            g_to = g_grouped[:].rearrange("p a c t -> p c a t")
+            nc.vector.tensor_copy(out=g_to[:, :, :VECTOR_TAPS], in_=g_from[:, :, :VECTOR_TAPS])
+            nc.scalar.copy(out=g_to[:, :, VECTOR_TAPS:], in_=g_from[:, :, VECTOR_TAPS:])
 
             g_codes = keep.tile([P, TAPS, P], U32, align_bytes=64, name="g_codes%d" % m)
             g_scales = keep.tile([P, TAPS, P], U8, align_bytes=64, name="g_scales%d" % m)

@@ -72,10 +72,10 @@ def tile_model_pa_s_kernel(tc, image, grad_output, grad_out, out):
         out_rows = out.rearrange("n c r q -> c n (r q)")
         for m in range(CI_TILES):
             g_grouped = keep.tile([P, TAPS, P, PACK], BF16, align_bytes=64, name="g_grouped%d" % m)
-            g_from = g_raw[m][:].rearrange("p t c a -> p c a t")
-            g_to = g_grouped[:].rearrange("p a c t -> p c a t")
-            nc.vector.tensor_copy(out=g_to[:, :, :VECTOR_TAPS], in_=g_from[:, :, :VECTOR_TAPS])
-            nc.scalar.copy(out=g_to[:, :, VECTOR_TAPS:], in_=g_from[:, :, VECTOR_TAPS:])
+            g_from = g_raw[m][:].rearrange("p t c a -> p c t a")
+            g_to = g_grouped[:].rearrange("p a c t -> p c t a")
+            nc.vector.tensor_copy(out=g_to[:, :, :, :VECTOR_TAPS], in_=g_from[:, :, :, :VECTOR_TAPS])
+            nc.scalar.copy(out=g_to[:, :, :, VECTOR_TAPS:], in_=g_from[:, :, :, VECTOR_TAPS:])
 
             g_codes = keep.tile([P, TAPS, P], U32, align_bytes=64, name="g_codes%d" % m)
             g_scales = keep.tile([P, TAPS, P], U8, align_bytes=64, name="g_scales%d" % m)

@@ -23,7 +23,10 @@ N_PASS = 512
 TAP_PITCH = 192
 Y_FILLED = TAPS * TAP_PITCH
 Y_COLS = (TAPS - 1) * TAP_PITCH + N_PASS
-VECTOR_TAPS = 3
+
+VECTOR_ROW, SHARED_ROW, SCALAR_ROW = 0, 1, 2
+SHARED_SPLIT = 80
+ROW_ORDER = (VECTOR_ROW, SCALAR_ROW, SHARED_ROW)
 
 FLOPS = 2 * CO * CI * TAPS * IMAGES * HO * WO
 BYTES = 2 * IMAGES * CO * HO * WO + 2 * CO * CI * TAPS + 4 * IMAGES * CI * H * W
@@ -34,14 +37,15 @@ def tile_model_pa_s_kernel(tc, image, grad_output, grad_out, out):
     with ExitStack() as ctx:
         keep = ctx.enter_context(tc.tile_pool(name="keep", bufs=1))
         psum = ctx.enter_context(tc.psum_pool(name="psum", bufs=1))
+        ctx.enter_context(tc.manual_schedule())
 
         y_raw = keep.tile([P, IMAGES, PACK, HO * WO], BF16)
         nc.sync.dma_start(out=y_raw[:], in_=grad_output.rearrange("n (p t) i j -> p n t (i j)", t=PACK))
-        g_rows = grad_out.rearrange("(p t) c kh kw -> p t c (kh kw)", t=PACK)
+        g_rows = grad_out.rearrange("(p t) c kh kw -> p t c kh kw", t=PACK)
         g_raw = []
         for m in range(CI_TILES):
-            g_raw.append(keep.tile([P, PACK, P, TAPS], BF16, name="g_raw%d" % m))
-            nc.sync.dma_start(out=g_raw[m][:], in_=g_rows[:, :, m * P : (m + 1) * P, :])
+            g_raw.append(keep.tile([P, PACK, P, KH, KW], BF16, name="g_raw%d" % m))
+            nc.sync.dma_start(out=g_raw[m][:], in_=g_rows[:, :, m * P : (m + 1) * P])
 
         y_shift = keep.tile([P, TAPS, TAP_PITCH, PACK], BF16, align_bytes=64)
         nc.vector.memset(y_shift[:], 0.0)
@@ -69,39 +73,62 @@ def tile_model_pa_s_kernel(tc, image, grad_output, grad_out, out):
                 in_=y_flat[:, first * PACK : last * PACK],
             )
 
-        out_rows = out.rearrange("n c r q -> c n (r q)")
+        g_grouped, g_codes, g_scales, acc = [], [], [], []
         for m in range(CI_TILES):
-            g_grouped = keep.tile([P, TAPS, P, PACK], BF16, align_bytes=64, name="g_grouped%d" % m)
-            g_from = g_raw[m][:].rearrange("p t c a -> p c t a")
-            g_to = g_grouped[:].rearrange("p a c t -> p c t a")
-            nc.vector.tensor_copy(out=g_to[:, :, :, :VECTOR_TAPS], in_=g_from[:, :, :, :VECTOR_TAPS])
-            nc.scalar.copy(out=g_to[:, :, :, VECTOR_TAPS:], in_=g_from[:, :, :, VECTOR_TAPS:])
+            g_grouped.append(keep.tile([P, KH, KW, P, PACK], BF16, align_bytes=64, name="g_grouped%d" % m))
+            g_codes.append(keep.tile([P, KH, KW, P], U32, align_bytes=64, name="g_codes%d" % m))
+            g_scales.append(keep.tile([P, KH, KW, P], U8, align_bytes=64, name="g_scales%d" % m))
+            acc.append(psum.tile([P, N_PASS], F32, name="acc%d" % m))
 
-            g_codes = keep.tile([P, TAPS, P], U32, align_bytes=64, name="g_codes%d" % m)
-            g_scales = keep.tile([P, TAPS, P], U8, align_bytes=64, name="g_scales%d" % m)
-            for kh in range(KH):
-                pair = slice(kh * KW, (kh + 1) * KW)
+        def regroup(m):
+            g_from = g_raw[m][:].rearrange("p t c kh kw -> p kh c t kw")
+            g_to = g_grouped[m][:].rearrange("p kh kw c t -> p kh c t kw")
+            nc.vector.tensor_copy(out=g_to[:, VECTOR_ROW], in_=g_from[:, VECTOR_ROW])
+            nc.vector.tensor_copy(
+                out=g_to[:, SHARED_ROW, :SHARED_SPLIT], in_=g_from[:, SHARED_ROW, :SHARED_SPLIT]
+            )
+            nc.scalar.copy(out=g_to[:, SCALAR_ROW], in_=g_from[:, SCALAR_ROW])
+            nc.scalar.copy(
+                out=g_to[:, SHARED_ROW, SHARED_SPLIT:], in_=g_from[:, SHARED_ROW, SHARED_SPLIT:]
+            )
+
+        def quantise(m):
+            for kh in ROW_ORDER:
                 nc.vector.quantize_mx(
-                    out=g_codes[:, pair, :].rearrange("p a c -> p (a c)").bitcast(E5M2_X4),
-                    scales=g_scales[:, pair, :].rearrange("p a c -> p (a c)"),
-                    in_=g_grouped[:, pair].rearrange("p a c t -> p (a c t)"),
+                    out=g_codes[m][:, kh].rearrange("p kw c -> p (kw c)").bitcast(E5M2_X4),
+                    scales=g_scales[m][:, kh].rearrange("p kw c -> p (kw c)"),
+                    in_=g_grouped[m][:, kh].rearrange("p kw c t -> p (kw c t)"),
                 )
 
-            acc = psum.tile([P, N_PASS], F32, name="acc%d" % m)
-            for tap in range(TAPS):
-                window = slice(tap * TAP_PITCH, tap * TAP_PITCH + N_PASS)
-                nc.tensor.matmul_mx(
-                    out=acc[:],
-                    lhsT=g_codes[:, tap, :].bitcast(E5M2_X4),
-                    lhsT_scale=g_scales[:, tap, :],
-                    rhs=y_codes[:, window].bitcast(E4M3_X4),
-                    rhs_scale=y_scales[:, window],
-                    start=(tap == 0),
-                    stop=(tap == TAPS - 1),
-                )
+        def multiply(m):
+            for kh in ROW_ORDER:
+                for kw in range(KW):
+                    first_col = (kh * KW + kw) * TAP_PITCH
+                    window = slice(first_col, first_col + N_PASS)
+                    nc.tensor.matmul_mx(
+                        out=acc[m][:],
+                        lhsT=g_codes[m][:, kh, kw, :].bitcast(E5M2_X4),
+                        lhsT_scale=g_scales[m][:, kh, kw, :],
+                        rhs=y_codes[:, window].bitcast(E4M3_X4),
+                        rhs_scale=y_scales[:, window],
+                        start=(kh == ROW_ORDER[0] and kw == 0),
+                        stop=(kh == ROW_ORDER[-1] and kw == KW - 1),
+                    )
+
+        out_rows = out.rearrange("n c r q -> c n (r q)")
+
+        def empty(m):
             result = keep.tile([P, OUT_COLS], F32, name="result%d" % m)
-            nc.scalar.copy(out=result[:], in_=acc[:, 0:OUT_COLS])
+            nc.scalar.copy(out=result[:], in_=acc[m][:, 0:OUT_COLS])
             nc.sync.dma_start(
                 out=out_rows[m * P : (m + 1) * P],
                 in_=result[:].rearrange("p (n g) -> p n g", n=IMAGES),
             )
+
+        for m in range(CI_TILES):
+            regroup(m)
+            if m > 0:
+                empty(m - 1)
+            quantise(m)
+            multiply(m)
+        empty(CI_TILES - 1)

@@ -18,15 +18,49 @@ KH, KW = 3, 2
 HO, WO = H - KH + 1, W - KW + 1
 TAPS = KH * KW
 CI_TILES = CI // P
-OUT_COLS = IMAGES * H * W
+GRID = H * W
+SLOTS = 4
+OUT_COLS = GRID * SLOTS
 N_PASS = 512
-TAP_PITCH = 192
-Y_FILLED = TAPS * TAP_PITCH
+TAP_PITCH = 384
 Y_COLS = (TAPS - 1) * TAP_PITCH + N_PASS
+KW_STEP = TAP_PITCH + SLOTS
+KH_STEP = KW * TAP_PITCH + W * SLOTS
 
-VECTOR_ROW, SHARED_ROW, SCALAR_ROW = 0, 1, 2
-SHARED_SPLIT = 80
-ROW_ORDER = (VECTOR_ROW, SCALAR_ROW, SHARED_ROW)
+LOADS = (((0, 64), (64, 64)), ((0, 128),), ((0, 128),), ((0, 128),))
+ORDER = (
+    ("V", "place", 0, 1),
+    ("S", "copy a", 0, 0),
+    ("V", "copy b", 0, 0),
+    ("S", "copy", 0, 2),
+    ("V", "place", 1, 3),
+    ("V", "quantise", 0, 0),
+    ("V", "copy", 0, 1),
+    ("V", "quantise", 0, 2),
+    ("V", "copy", 1, 0),
+    ("S", "copy", 1, 1),
+    ("V", "quantise", 0, 1),
+    ("V", "quantise", 1, 0),
+    ("V", "copy", 1, 2),
+    ("S", "copy", 2, 0),
+    ("S", "empty", 0, 0),
+    ("V", "quantise", 1, 1),
+    ("V", "quantise", 1, 2),
+    ("V", "copy", 2, 1),
+    ("S", "copy", 2, 2),
+    ("S", "empty", 1, 0),
+    ("V", "quantise", 2, 0),
+    ("V", "quantise", 2, 1),
+    ("V", "copy", 3, 0),
+    ("V", "copy", 3, 2),
+    ("S", "copy", 3, 1),
+    ("V", "quantise", 2, 2),
+    ("V", "quantise", 3, 0),
+    ("V", "quantise", 3, 2),
+    ("S", "empty", 2, 0),
+    ("V", "quantise", 3, 1),
+    ("S", "empty", 3, 0),
+)
 
 FLOPS = 2 * CO * CI * TAPS * IMAGES * HO * WO
 BYTES = 2 * IMAGES * CO * HO * WO + 2 * CO * CI * TAPS + 4 * IMAGES * CI * H * W
@@ -39,38 +73,54 @@ def tile_model_pa_s_kernel(tc, image, grad_output, grad_out, out):
         psum = ctx.enter_context(tc.psum_pool(name="psum", bufs=1))
         ctx.enter_context(tc.manual_schedule())
 
+        warm = keep.tile([P, 2], F32)
+        nc.gpsimd.memset(warm[:, 0:1], 0.0)
+        nc.scalar.copy(out=warm[:, 1:2], in_=warm[:, 0:1])
+
         y_raw = keep.tile([P, IMAGES, PACK, HO * WO], BF16)
         nc.sync.dma_start(out=y_raw[:], in_=grad_output.rearrange("n (p t) i j -> p n t (i j)", t=PACK))
         g_rows = grad_out.rearrange("(p t) c kh kw -> p t c kh kw", t=PACK)
         g_raw = []
         for m in range(CI_TILES):
-            g_raw.append(keep.tile([P, PACK, P, KH, KW], BF16, name="g_raw%d" % m))
-            nc.sync.dma_start(out=g_raw[m][:], in_=g_rows[:, :, m * P : (m + 1) * P])
+            g_raw.append([])
+            for c0, width in LOADS[m]:
+                part = keep.tile([P, PACK, width, KH, KW], BF16, name="g_raw%d_%d" % (m, c0))
+                nc.sync.dma_start(out=part[:], in_=g_rows[:, :, m * P + c0 : m * P + c0 + width])
+                g_raw[m].append((c0, width, part))
 
-        y_shift = keep.tile([P, TAPS, TAP_PITCH, PACK], BF16, align_bytes=64)
-        nc.vector.memset(y_shift[:], 0.0)
-        y_codes = keep.tile([P, Y_COLS], U32, align_bytes=64)
+        y_pad = keep.tile([P, HO * WO, SLOTS, PACK], BF16, align_bytes=64)
+        nc.vector.memset(y_pad[:], 0.0)
+        y_codes = keep.tile([P, Y_COLS], I32, align_bytes=64)
         y_scales = keep.tile([P, Y_COLS], U8, align_bytes=64)
-        nc.vector.memset(y_codes[:, Y_FILLED:].bitcast(I32), 0)
-        nc.vector.memset(y_scales[:, Y_FILLED:].bitcast(I32), 0)
+        nc.vector.memset(y_scales[:].bitcast(I32), 0)
+        nc.vector.memset(y_codes[:, 0 : Y_COLS // 2], 0)
+        nc.gpsimd.memset(y_codes[:, Y_COLS // 2 :].bitcast(F32), 0.0)
+        nc.scalar.copy(out=y_pad[:, :, 0:IMAGES, :], in_=y_raw[:].rearrange("p n t l -> p l n t"))
+        yq_codes = keep.tile([P, HO * WO * SLOTS], I32, align_bytes=64)
+        yq_scales = keep.tile([P, HO * WO * SLOTS], U8, align_bytes=64)
+        nc.vector.quantize_mx(
+            out=yq_codes[:].bitcast(E4M3_X4),
+            scales=yq_scales[:],
+            in_=y_pad[:].rearrange("p l s t -> p (l s t)"),
+        )
 
-        y_grouped = keep.tile([P, IMAGES, HO * WO, PACK], BF16)
-        nc.vector.tensor_copy(out=y_grouped[:], in_=y_raw[:].rearrange("p n t l -> p n l t"))
-        y_lines = y_grouped[:].rearrange("p n (i j) t -> p n i (j t)", i=HO)
-        for kh in range(KH):
-            for kw in range(KW):
-                grid = y_shift[:, kh * KW + kw, 0:OUT_COLS, :].rearrange(
-                    "p (n r q) t -> p n r (q t)", n=IMAGES, r=H
-                )
-                nc.vector.tensor_copy(
-                    out=grid[:, :, kh : kh + HO, kw * PACK : (kw + WO) * PACK], in_=y_lines
-                )
-        y_flat = y_shift[:].rearrange("p a c t -> p (a c t)")
-        for first, last in ((0, 1024), (1024, Y_FILLED)):
-            nc.vector.quantize_mx(
-                out=y_codes[:, first:last].bitcast(E4M3_X4),
-                scales=y_scales[:, first:last],
-                in_=y_flat[:, first * PACK : last * PACK],
+        def shifted(flat, unit):
+            v = flat[:, 0 : KH * KH_STEP // unit].rearrange("p (kh a) -> p kh a", kh=KH)
+            v = v[:, :, 0 : KW * KW_STEP // unit].rearrange("p kh (kw b) -> p kh kw b", kw=KW)
+            v = v[:, :, :, 0 : HO * W * SLOTS // unit].rearrange("p kh kw (i w) -> p kh kw i w", i=HO)
+            return v[:, :, :, :, 0 : WO * SLOTS // unit]
+
+        def repeated(flat, unit):
+            v = flat.rearrange("p (i w) -> p i w", i=HO).unsqueeze(1).unsqueeze(1)
+            return v.to_broadcast([P, KH, KW, HO, WO * SLOTS // unit])
+
+        def place(kh0, kh1):
+            nc.vector.tensor_copy(
+                out=shifted(y_codes[:], 1)[:, kh0:kh1], in_=repeated(yq_codes[:], 1)[:, kh0:kh1]
+            )
+            nc.vector.tensor_copy(
+                out=shifted(y_scales[:].bitcast(I32), 4)[:, kh0:kh1],
+                in_=repeated(yq_scales[:].bitcast(I32), 4)[:, kh0:kh1],
             )
 
         g_grouped, g_codes, g_scales, acc = [], [], [], []
@@ -80,55 +130,59 @@ def tile_model_pa_s_kernel(tc, image, grad_output, grad_out, out):
             g_scales.append(keep.tile([P, KH, KW, P], U8, align_bytes=64, name="g_scales%d" % m))
             acc.append(psum.tile([P, N_PASS], F32, name="acc%d" % m))
 
-        def regroup(m):
-            g_from = g_raw[m][:].rearrange("p t c kh kw -> p kh c t kw")
+        def regroup(engine_copy, m, kh, loads):
             g_to = g_grouped[m][:].rearrange("p kh kw c t -> p kh c t kw")
-            nc.vector.tensor_copy(out=g_to[:, VECTOR_ROW], in_=g_from[:, VECTOR_ROW])
-            nc.vector.tensor_copy(
-                out=g_to[:, SHARED_ROW, :SHARED_SPLIT], in_=g_from[:, SHARED_ROW, :SHARED_SPLIT]
-            )
-            nc.scalar.copy(out=g_to[:, SCALAR_ROW], in_=g_from[:, SCALAR_ROW])
-            nc.scalar.copy(
-                out=g_to[:, SHARED_ROW, SHARED_SPLIT:], in_=g_from[:, SHARED_ROW, SHARED_SPLIT:]
-            )
-
-        def quantise(m):
-            for kh in ROW_ORDER:
-                nc.vector.quantize_mx(
-                    out=g_codes[m][:, kh].rearrange("p kw c -> p (kw c)").bitcast(E5M2_X4),
-                    scales=g_scales[m][:, kh].rearrange("p kw c -> p (kw c)"),
-                    in_=g_grouped[m][:, kh].rearrange("p kw c t -> p (kw c t)"),
+            for c0, width, part in g_raw[m][loads]:
+                engine_copy(
+                    out=g_to[:, kh, c0 : c0 + width],
+                    in_=part[:].rearrange("p t c kh kw -> p kh c t kw")[:, kh],
                 )
 
-        def multiply(m):
-            for kh in ROW_ORDER:
-                for kw in range(KW):
-                    first_col = (kh * KW + kw) * TAP_PITCH
-                    window = slice(first_col, first_col + N_PASS)
-                    nc.tensor.matmul_mx(
-                        out=acc[m][:],
-                        lhsT=g_codes[m][:, kh, kw, :].bitcast(E5M2_X4),
-                        lhsT_scale=g_scales[m][:, kh, kw, :],
-                        rhs=y_codes[:, window].bitcast(E4M3_X4),
-                        rhs_scale=y_scales[:, window],
-                        start=(kh == ROW_ORDER[0] and kw == 0),
-                        stop=(kh == ROW_ORDER[-1] and kw == KW - 1),
-                    )
+        def quantise(m, kh):
+            nc.vector.quantize_mx(
+                out=g_codes[m][:, kh].rearrange("p kw c -> p (kw c)").bitcast(E5M2_X4),
+                scales=g_scales[m][:, kh].rearrange("p kw c -> p (kw c)"),
+                in_=g_grouped[m][:, kh].rearrange("p kw c t -> p (kw c t)"),
+            )
+
+        passes_done = [0] * CI_TILES
+
+        def multiply(m, kh):
+            for kw in range(KW):
+                first_col = (kh * KW + kw) * TAP_PITCH
+                window = slice(first_col, first_col + N_PASS)
+                nc.tensor.matmul_mx(
+                    out=acc[m][:],
+                    lhsT=g_codes[m][:, kh, kw, :].bitcast(E5M2_X4),
+                    lhsT_scale=g_scales[m][:, kh, kw, :],
+                    rhs=y_codes[:, window].bitcast(E4M3_X4),
+                    rhs_scale=y_scales[:, window],
+                    start=(passes_done[m] == 0),
+                    stop=(passes_done[m] == TAPS - 1),
+                )
+                passes_done[m] += 1
 
         out_rows = out.rearrange("n c r q -> c n (r q)")
 
         def empty(m):
-            result = keep.tile([P, OUT_COLS], F32, name="result%d" % m)
-            nc.scalar.copy(out=result[:], in_=acc[m][:, 0:OUT_COLS])
-            nc.sync.dma_start(
-                out=out_rows[m * P : (m + 1) * P],
-                in_=result[:].rearrange("p (n g) -> p n g", n=IMAGES),
+            result = keep.tile([P, IMAGES, GRID], F32, name="result%d" % m)
+            nc.scalar.copy(
+                out=result[:],
+                in_=acc[m][:, 0:OUT_COLS].rearrange("p (g s) -> p s g", s=SLOTS)[:, 0:IMAGES, :],
             )
+            nc.sync.dma_start(out=out_rows[m * P : (m + 1) * P], in_=result[:])
 
-        for m in range(CI_TILES):
-            regroup(m)
-            if m > 0:
-                empty(m - 1)
-            quantise(m)
-            multiply(m)
-        empty(CI_TILES - 1)
+        for engine, what, m, kh in ORDER:
+            if what == "copy":
+                regroup(nc.scalar.copy if engine == "S" else nc.vector.tensor_copy, m, kh, slice(0, 2))
+            elif what == "copy a":
+                regroup(nc.scalar.copy if engine == "S" else nc.vector.tensor_copy, m, kh, slice(0, 1))
+            elif what == "copy b":
+                regroup(nc.scalar.copy if engine == "S" else nc.vector.tensor_copy, m, kh, slice(1, 2))
+            elif what == "place":
+                place(m, kh)
+            elif what == "quantise":
+                quantise(m, kh)
+                multiply(m, kh)
+            else:
+                empty(m)

@@ -27,7 +27,7 @@ Y_COLS = (TAPS - 1) * TAP_PITCH + N_PASS
 KW_STEP = TAP_PITCH + SLOTS
 KH_STEP = KW * TAP_PITCH + W * SLOTS
 
-LOADS = (((0, 64), (64, 64)), ((0, 128),), ((0, 128),), ((0, 128),))
+LOADS = (((0, 64), (64, 64)), ((0, 128),), ((0, 128),), ((0, 64), (64, 64)))
 ORDER = (
     ("V", "place", 0, 1),
     ("S", "copy a", 0, 0),
@@ -51,14 +51,17 @@ ORDER = (
     ("S", "empty", 1, 0),
     ("V", "quantise", 2, 0),
     ("V", "quantise", 2, 1),
-    ("V", "copy", 3, 0),
-    ("V", "copy", 3, 2),
-    ("S", "copy", 3, 1),
+    ("V", "copy a", 3, 0),
+    ("S", "copy a", 3, 1),
+    ("V", "copy a", 3, 2),
     ("V", "quantise", 2, 2),
+    ("V", "copy b", 3, 0),
+    ("S", "copy b", 3, 1),
     ("V", "quantise", 3, 0),
-    ("V", "quantise", 3, 2),
+    ("V", "copy b", 3, 2),
     ("S", "empty", 2, 0),
     ("V", "quantise", 3, 1),
+    ("V", "quantise", 3, 2),
     ("S", "empty", 3, 0),
 )
 

@@ -1,6 +1,7 @@
 from contextlib import ExitStack
 
 import concourse.mybir as mybir
+from concourse.masks import make_identity
 
 BF16 = mybir.dt.bfloat16
 F32 = mybir.dt.float32
@@ -29,6 +30,8 @@ KH_STEP = KW * TAP_PITCH + W * SLOTS
 
 LOADS = (((0, 64), (64, 64)), ((0, 128),), ((0, 128),), ((0, 64), (64, 64)))
 ORDER = (
+    ("T", "heat a", 2, 2),
+    ("T", "heat b", 2, 9),
     ("V", "place", 0, 1),
     ("S", "copy a", 0, 0),
     ("V", "copy b", 0, 0),
@@ -57,11 +60,11 @@ ORDER = (
     ("V", "quantise", 2, 2),
     ("V", "copy b", 3, 0),
     ("S", "copy b", 3, 1),
-    ("V", "quantise", 3, 0),
     ("V", "copy b", 3, 2),
+    ("V", "quantise", 3, 0),
     ("S", "empty", 2, 0),
-    ("V", "quantise", 3, 1),
     ("V", "quantise", 3, 2),
+    ("V", "quantise", 3, 1),
     ("S", "empty", 3, 0),
 )
 
@@ -79,6 +82,8 @@ def tile_model_pa_s_kernel(tc, image, grad_output, grad_out, out):
         warm = keep.tile([P, 2], F32)
         nc.gpsimd.memset(warm[:, 0:1], 0.0)
         nc.scalar.copy(out=warm[:, 1:2], in_=warm[:, 0:1])
+        ident = keep.tile([P, P], BF16)
+        make_identity(nc, ident[:])
 
         y_raw = keep.tile([P, IMAGES, PACK, HO * WO], BF16)
         nc.sync.dma_start(out=y_raw[:], in_=grad_output.rearrange("n (p t) i j -> p n t (i j)", t=PACK))
@@ -148,6 +153,23 @@ def tile_model_pa_s_kernel(tc, image, grad_output, grad_out, out):
                 in_=g_grouped[m][:, kh].rearrange("p kw c t -> p (kw c t)"),
             )
 
+        idle_bank = psum.tile([P, 8 * P], BF16)
+
+        def heat(load, matmuls, transposes):
+            flat = g_raw[0][load][2][:].rearrange("p t c kh kw -> p (t c kh kw)")
+            for i in range(matmuls):
+                nc.tensor.matmul(
+                    out=idle_bank[:, i * 2 * P : (i + 1) * 2 * P],
+                    lhsT=ident[:],
+                    rhs=flat[:, i * 2 * P : (i + 1) * 2 * P],
+                    start=True,
+                    stop=True,
+                )
+            for i in range(transposes):
+                nc.tensor.transpose(
+                    idle_bank[:, (i % 8) * P : (i % 8 + 1) * P], flat[:, (i % 8) * P : (i % 8 + 1) * P], ident[:]
+                )
+
         passes_done = [0] * CI_TILES
 
         def multiply(m, kh):
@@ -184,6 +206,10 @@ def tile_model_pa_s_kernel(tc, image, grad_output, grad_out, out):
                 regroup(nc.scalar.copy if engine == "S" else nc.vector.tensor_copy, m, kh, slice(1, 2))
             elif what == "place":
                 place(m, kh)
+            elif what == "heat a":
+                heat(0, m, kh)
+            elif what == "heat b":
+                heat(1, m, kh)
             elif what == "quantise":
                 quantise(m, kh)
                 multiply(m, kh)

@@ -19,24 +19,24 @@ KH, KW = 3, 2
 HO, WO = H - KH + 1, W - KW + 1
 TAPS = KH * KW
 CI_TILES = CI // P
-GRID = H * W
-SLOTS = 4
-OUT_COLS = GRID * SLOTS
 N_PASS = 512
-TAP_PITCH = 384
-Y_COLS = (TAPS - 1) * TAP_PITCH + N_PASS
-KW_STEP = TAP_PITCH + SLOTS
-KH_STEP = KW * TAP_PITCH + W * SLOTS
+FOLDS = 2
+ROWS = H // FOLDS
+BLOCK = 64
+SLOTS = IMAGES * FOLDS
+BUF_BLOCKS = ROWS + KH - 1
+KW_PITCH = BUF_BLOCKS * BLOCK
+Y_COLS = (KW - 1) * KW_PITCH + (KH - 1) * BLOCK + N_PASS
+KW_STEP = KW_PITCH + SLOTS
+QUANT_BLOCKS = 8
 
 LOADS = (((0, 64), (64, 64)), ((0, 128),), ((0, 128),), ((0, 64), (64, 64)))
 ORDER = (
     ("T", "heat a", 2, 2),
     ("T", "heat b", 2, 9),
-    ("V", "place", 0, 1),
     ("S", "copy a", 0, 0),
     ("V", "copy b", 0, 0),
     ("S", "copy", 0, 2),
-    ("V", "place", 1, 3),
     ("V", "quantise", 0, 0),
     ("V", "copy", 0, 1),
     ("V", "quantise", 0, 2),
@@ -96,40 +96,41 @@ def tile_model_pa_s_kernel(tc, image, grad_output, grad_out, out):
                 nc.sync.dma_start(out=part[:], in_=g_rows[:, :, m * P + c0 : m * P + c0 + width])
                 g_raw[m].append((c0, width, part))
 
-        y_pad = keep.tile([P, HO * WO, SLOTS, PACK], BF16, align_bytes=64)
+        y_pad = keep.tile([P, QUANT_BLOCKS, WO, IMAGES, FOLDS, PACK], BF16, align_bytes=64)
         nc.vector.memset(y_pad[:], 0.0)
         y_codes = keep.tile([P, Y_COLS], I32, align_bytes=64)
         y_scales = keep.tile([P, Y_COLS], U8, align_bytes=64)
         nc.vector.memset(y_scales[:].bitcast(I32), 0)
-        nc.vector.memset(y_codes[:, 0 : Y_COLS // 2], 0)
-        nc.gpsimd.memset(y_codes[:, Y_COLS // 2 :].bitcast(F32), 0.0)
-        nc.scalar.copy(out=y_pad[:, :, 0:IMAGES, :], in_=y_raw[:].rearrange("p n t l -> p l n t"))
-        yq_codes = keep.tile([P, HO * WO * SLOTS], I32, align_bytes=64)
-        yq_scales = keep.tile([P, HO * WO * SLOTS], U8, align_bytes=64)
+        nc.gpsimd.memset(y_codes[:].bitcast(F32), 0.0)
+        for fold, engine_copy in ((0, nc.vector.tensor_copy), (1, nc.scalar.copy)):
+            i0 = fold * (HO - ROWS)
+            g0 = i0 - ROWS * fold + KH - 1
+            engine_copy(
+                out=y_pad[:, g0 : g0 + ROWS, :, :, fold, :].rearrange("p g j n t -> p (g j) n t"),
+                in_=y_raw[:, :, :, i0 * WO : (i0 + ROWS) * WO].rearrange("p n t l -> p l n t"),
+            )
+        y_quant_cols = QUANT_BLOCKS * WO * SLOTS
+        yq_codes = keep.tile([P, y_quant_cols], I32, align_bytes=64)
+        yq_scales = keep.tile([P, y_quant_cols], U8, align_bytes=64)
         nc.vector.quantize_mx(
             out=yq_codes[:].bitcast(E4M3_X4),
             scales=yq_scales[:],
-            in_=y_pad[:].rearrange("p l s t -> p (l s t)"),
+            in_=y_pad[:].rearrange("p g j n f t -> p (g j n f t)"),
         )
 
-        def shifted(flat, unit):
-            v = flat[:, 0 : KH * KH_STEP // unit].rearrange("p (kh a) -> p kh a", kh=KH)
-            v = v[:, :, 0 : KW * KW_STEP // unit].rearrange("p kh (kw b) -> p kh kw b", kw=KW)
-            v = v[:, :, :, 0 : HO * W * SLOTS // unit].rearrange("p kh kw (i w) -> p kh kw i w", i=HO)
-            return v[:, :, :, :, 0 : WO * SLOTS // unit]
+        def buffers(flat, unit):
+            v = flat[:, 0 : KW * KW_STEP // unit].rearrange("p (kw a) -> p kw a", kw=KW)
+            v = v[:, :, 0 : KW_PITCH // unit].rearrange("p kw (g w) -> p kw g w", g=BUF_BLOCKS)
+            return v[:, :, :, 0 : WO * SLOTS // unit]
 
         def repeated(flat, unit):
-            v = flat.rearrange("p (i w) -> p i w", i=HO).unsqueeze(1).unsqueeze(1)
-            return v.to_broadcast([P, KH, KW, HO, WO * SLOTS // unit])
+            v = flat[:, 0 : BUF_BLOCKS * WO * SLOTS // unit].rearrange("p (g w) -> p g w", g=BUF_BLOCKS)
+            return v.unsqueeze(1).to_broadcast([P, KW, BUF_BLOCKS, WO * SLOTS // unit])
 
-        def place(kh0, kh1):
-            nc.vector.tensor_copy(
-                out=shifted(y_codes[:], 1)[:, kh0:kh1], in_=repeated(yq_codes[:], 1)[:, kh0:kh1]
-            )
-            nc.vector.tensor_copy(
-                out=shifted(y_scales[:].bitcast(I32), 4)[:, kh0:kh1],
-                in_=repeated(yq_scales[:].bitcast(I32), 4)[:, kh0:kh1],
-            )
+        nc.vector.tensor_copy(out=buffers(y_codes[:], 1), in_=repeated(yq_codes[:], 1))
+        nc.vector.tensor_copy(
+            out=buffers(y_scales[:].bitcast(I32), 4), in_=repeated(yq_scales[:].bitcast(I32), 4)
+        )
 
         g_grouped, g_codes, g_scales, acc = [], [], [], []
         for m in range(CI_TILES):
@@ -174,7 +175,7 @@ def tile_model_pa_s_kernel(tc, image, grad_output, grad_out, out):
 
         def multiply(m, kh):
             for kw in range(KW):
-                first_col = (kh * KW + kw) * TAP_PITCH
+                first_col = kw * KW_PITCH + (KH - 1 - kh) * BLOCK
                 window = slice(first_col, first_col + N_PASS)
                 nc.tensor.matmul_mx(
                     out=acc[m][:],
@@ -190,12 +191,17 @@ def tile_model_pa_s_kernel(tc, image, grad_output, grad_out, out):
         out_rows = out.rearrange("n c r q -> c n (r q)")
 
         def empty(m):
-            result = keep.tile([P, IMAGES, GRID], F32, name="result%d" % m)
+            result = keep.tile([P, SLOTS, ROWS, W], F32, name="result%d" % m)
             nc.scalar.copy(
                 out=result[:],
-                in_=acc[m][:, 0:OUT_COLS].rearrange("p (g s) -> p s g", s=SLOTS)[:, 0:IMAGES, :],
+                in_=acc[m][:, 0 : ROWS * BLOCK]
+                .rearrange("p (b w) -> p b w", w=BLOCK)[:, :, 0 : W * SLOTS]
+                .rearrange("p b (q s) -> p s b q", s=SLOTS),
             )
-            nc.sync.dma_start(out=out_rows[m * P : (m + 1) * P], in_=result[:])
+            nc.sync.dma_start(
+                out=out_rows[m * P : (m + 1) * P],
+                in_=result[:].rearrange("p (n f) b q -> p n (f b q)", f=FOLDS),
+            )
 
         for engine, what, m, kh in ORDER:
             if what == "copy":
@@ -204,8 +210,6 @@ def tile_model_pa_s_kernel(tc, image, grad_output, grad_out, out):
                 regroup(nc.scalar.copy if engine == "S" else nc.vector.tensor_copy, m, kh, slice(0, 1))
             elif what == "copy b":
                 regroup(nc.scalar.copy if engine == "S" else nc.vector.tensor_copy, m, kh, slice(1, 2))
-            elif what == "place":
-                place(m, kh)
             elif what == "heat a":
                 heat(0, m, kh)
             elif what == "heat b":

@@ -22,6 +22,7 @@ CI_TILES = CI // P
 N_PASS = 512
 FOLDS = 2
 ROWS = H // FOLDS
+GRID = H * W
 BLOCK = 64
 SLOTS = IMAGES * FOLDS
 BUF_BLOCKS = ROWS + KH - 1
@@ -31,6 +32,9 @@ KW_STEP = KW_PITCH + SLOTS
 QUANT_BLOCKS = 8
 
 LOADS = (((0, 64), (64, 64)), ((0, 128),), ((0, 128),), ((0, 64), (64, 64)))
+KH_ORDER = ((0, 2, 1), (0, 1, 2), (0, 1, 2), (0, 2, 1))
+EXTRA = 6
+HEAD = (0, 96, 184, 272, 360)
 ORDER = (
     ("T", "heat a", 2, 2),
     ("T", "heat b", 2, 9),
@@ -53,19 +57,32 @@ ORDER = (
     ("S", "copy", 2, 2),
     ("S", "empty", 1, 0),
     ("V", "quantise", 2, 0),
+    ("T", "borrow", 0, 0),
     ("V", "quantise", 2, 1),
     ("V", "copy a", 3, 0),
     ("S", "copy a", 3, 1),
+    ("S", "append", 0, 0),
+    ("D", "store", 0, 0),
     ("V", "copy a", 3, 2),
     ("V", "quantise", 2, 2),
+    ("T", "borrow", 1, 0),
     ("V", "copy b", 3, 0),
     ("S", "copy b", 3, 1),
+    ("S", "append", 1, 0),
+    ("D", "store", 1, 0),
     ("V", "copy b", 3, 2),
     ("V", "quantise", 3, 0),
     ("S", "empty", 2, 0),
-    ("V", "quantise", 3, 2),
-    ("V", "quantise", 3, 1),
     ("S", "empty", 3, 0),
+    ("V", "quantise", 3, 2),
+    ("T", "borrow", 2, 0),
+    ("T", "borrow", 3, 0),
+    ("S", "append", 2, 0),
+    ("D", "store", 2, 0),
+    ("S", "append", 3, 0),
+    ("V", "quantise", 3, 1),
+    ("V", "finish", 3, 0),
+    ("D", "store", 3, 0),
 )
 
 FLOPS = 2 * CO * CI * TAPS * IMAGES * HO * WO
@@ -82,8 +99,12 @@ def tile_model_pa_s_kernel(tc, image, grad_output, grad_out, out):
         warm = keep.tile([P, 2], F32)
         nc.gpsimd.memset(warm[:, 0:1], 0.0)
         nc.scalar.copy(out=warm[:, 1:2], in_=warm[:, 0:1])
+        wide = keep.tile([P, P + 1], F32)
+        make_identity(nc, wide[:, 0:P])
+        nc.gpsimd.memset(wide[:, P : P + 1], 0.0)
+        shift = wide[:, 1 : P + 1]
         ident = keep.tile([P, P], BF16)
-        make_identity(nc, ident[:])
+        nc.vector.tensor_copy(out=ident[:], in_=wide[:, 0:P])
 
         y_raw = keep.tile([P, IMAGES, PACK, HO * WO], BF16)
         nc.sync.dma_start(out=y_raw[:], in_=grad_output.rearrange("n (p t) i j -> p n t (i j)", t=PACK))
@@ -138,6 +159,7 @@ def tile_model_pa_s_kernel(tc, image, grad_output, grad_out, out):
             g_codes.append(keep.tile([P, KH, KW, P], U32, align_bytes=64, name="g_codes%d" % m))
             g_scales.append(keep.tile([P, KH, KW, P], U8, align_bytes=64, name="g_scales%d" % m))
             acc.append(psum.tile([P, N_PASS], F32, name="acc%d" % m))
+        acc_rest = psum.tile([P, N_PASS], F32)
 
         def regroup(engine_copy, m, kh, loads):
             g_to = g_grouped[m][:].rearrange("p kh kw c t -> p kh c t kw")
@@ -171,37 +193,66 @@ def tile_model_pa_s_kernel(tc, image, grad_output, grad_out, out):
                     idle_bank[:, (i % 8) * P : (i % 8 + 1) * P], flat[:, (i % 8) * P : (i % 8 + 1) * P], ident[:]
                 )
 
-        passes_done = [0] * CI_TILES
-
         def multiply(m, kh):
+            apart = m == CI_TILES - 1
+            last = KH_ORDER[m][-1]
+            to = acc_rest if apart and kh > 0 else acc[m]
             for kw in range(KW):
                 first_col = kw * KW_PITCH + (KH - 1 - kh) * BLOCK
                 window = slice(first_col, first_col + N_PASS)
                 nc.tensor.matmul_mx(
-                    out=acc[m][:],
+                    out=to[:],
                     lhsT=g_codes[m][:, kh, kw, :].bitcast(E5M2_X4),
                     lhsT_scale=g_scales[m][:, kh, kw, :],
                     rhs=y_codes[:, window].bitcast(E4M3_X4),
                     rhs_scale=y_scales[:, window],
-                    start=(passes_done[m] == 0),
-                    stop=(passes_done[m] == TAPS - 1),
+                    start=(kw == 0 and kh in (KH_ORDER[m][0], KH_ORDER[m][1] if apart else KH_ORDER[m][0])),
+                    stop=(kw == KW - 1 and kh in (last, KH_ORDER[m][0] if apart else last)),
                 )
-                passes_done[m] += 1
 
-        out_rows = out.rearrange("n c r q -> c n (r q)")
+        out_rows = out.rearrange("n (c k) r q -> c n (k r q)", k=4)
+        result, part, extra = [], [], []
+
+        def row_view(bank, n):
+            v = bank[:, 0 : ROWS * BLOCK].rearrange("p (b w) -> p b w", w=BLOCK)[:, :, 0 : W * SLOTS]
+            return v.rearrange("p b (q s) -> p s b q", s=SLOTS)[:, n * FOLDS : (n + 1) * FOLDS]
 
         def empty(m):
-            result = keep.tile([P, SLOTS, ROWS, W], F32, name="result%d" % m)
+            result.append(keep.tile([P, IMAGES, GRID + EXTRA], F32, name="result%d" % m))
+            for n in range(IMAGES):
+                nc.scalar.copy(
+                    out=result[m][:, n, 0:GRID].rearrange("p (f b q) -> p f b q", f=FOLDS, b=ROWS),
+                    in_=row_view(acc[m], n),
+                )
+
+        def borrow(m):
+            extra.append(psum.tile([P, N_PASS], F32, name="extra%d" % (m % 2)))
+            nc.tensor.matmul(
+                out=extra[m][:, 0 : IMAGES * EXTRA],
+                lhsT=shift,
+                rhs=result[m][:, :, 0:EXTRA],
+                start=True,
+                stop=True,
+            )
+
+        def append(m):
             nc.scalar.copy(
-                out=result[:],
-                in_=acc[m][:, 0 : ROWS * BLOCK]
-                .rearrange("p (b w) -> p b w", w=BLOCK)[:, :, 0 : W * SLOTS]
-                .rearrange("p b (q s) -> p s b q", s=SLOTS),
+                out=result[m][:, :, GRID : GRID + EXTRA],
+                in_=extra[m][:, 0 : IMAGES * EXTRA].rearrange("p (n e) -> p n e", n=IMAGES),
             )
-            nc.sync.dma_start(
-                out=out_rows[m * P : (m + 1) * P],
-                in_=result[:].rearrange("p (n f) b q -> p n (f b q)", f=FOLDS),
-            )
+
+        def store(m):
+            for k in range(4):
+                own = HEAD[k] - k * GRID
+                nc.sync.dma_start(
+                    out=out_rows[m * P // 4 : (m + 1) * P // 4, :, HEAD[k] : HEAD[k + 1]],
+                    in_=result[m][k:P:4, :, own : own + HEAD[k + 1] - HEAD[k]],
+                )
+
+        def finish(m):
+            for n in range(IMAGES):
+                v = result[m][:, n, 0:GRID].rearrange("p (f b q) -> p f b q", f=FOLDS, b=ROWS)
+                nc.vector.tensor_add(out=v, in0=row_view(acc_rest, n), in1=v)
 
         for engine, what, m, kh in ORDER:
             if what == "copy":
@@ -217,5 +268,13 @@ def tile_model_pa_s_kernel(tc, image, grad_output, grad_out, out):
             elif what == "quantise":
                 quantise(m, kh)
                 multiply(m, kh)
-            else:
+            elif what == "empty":
                 empty(m)
+            elif what == "borrow":
+                borrow(m)
+            elif what == "append":
+                append(m)
+            elif what == "store":
+                store(m)
+            else:
+                finish(m)

@@ -31,56 +31,60 @@ Y_COLS = (KW - 1) * KW_PITCH + (KH - 1) * BLOCK + N_PASS
 KW_STEP = KW_PITCH + SLOTS
 QUANT_BLOCKS = 8
 
-LOADS = (((0, 64), (64, 64)), ((0, 128),), ((0, 128),), ((0, 64), (64, 64)))
-KH_ORDER = ((0, 2, 1), (0, 1, 2), (0, 1, 2), (0, 2, 1))
+LOADS = (((0, 64), (64, 64)),) * CI_TILES
+KH_ORDER = ((0, 1, 2), (0, 1, 2), (0, 1, 2), (0, 1, 2))
+TENSOR_ROW = 2
 EXTRA = 6
 HEAD = (0, 96, 184, 272, 360)
 ORDER = (
-    ("T", "heat a", 2, 2),
-    ("T", "heat b", 2, 9),
+    ("T", "regroup", 0, 0),
+    ("T", "regroup", 0, 1),
+    ("T", "heat", 0, 9),
     ("S", "copy a", 0, 0),
+    ("S", "copy a", 0, 1),
     ("V", "copy b", 0, 0),
-    ("S", "copy", 0, 2),
+    ("V", "copy b", 0, 1),
+    ("S", "fetch", 0, 2),
     ("V", "quantise", 0, 0),
-    ("V", "copy", 0, 1),
-    ("V", "quantise", 0, 2),
-    ("V", "copy", 1, 0),
-    ("S", "copy", 1, 1),
+    ("V", "copy a", 1, 0),
+    ("S", "copy a", 1, 1),
     ("V", "quantise", 0, 1),
+    ("V", "copy b", 1, 0),
+    ("S", "copy b", 1, 1),
+    ("V", "quantise", 0, 2),
+    ("V", "copy a", 1, 2),
+    ("S", "copy b", 1, 2),
     ("V", "quantise", 1, 0),
-    ("V", "copy", 1, 2),
-    ("S", "copy", 2, 0),
-    ("S", "empty", 0, 0),
     ("V", "quantise", 1, 1),
+    ("V", "copy a", 2, 0),
+    ("S", "copy a", 2, 1),
     ("V", "quantise", 1, 2),
-    ("V", "copy", 2, 1),
-    ("S", "copy", 2, 2),
-    ("S", "empty", 1, 0),
+    ("V", "copy b", 2, 0),
+    ("S", "copy b", 2, 1),
+    ("S", "empty", 0, 0),
+    ("D", "store rows", 0, 0),
+    ("V", "copy a", 2, 2),
+    ("S", "copy b", 2, 2),
     ("V", "quantise", 2, 0),
-    ("T", "borrow", 0, 0),
     ("V", "quantise", 2, 1),
     ("V", "copy a", 3, 0),
     ("S", "copy a", 3, 1),
-    ("S", "append", 0, 0),
-    ("D", "store", 0, 0),
-    ("V", "copy a", 3, 2),
+    ("S", "empty", 1, 0),
+    ("D", "store rows", 1, 0),
     ("V", "quantise", 2, 2),
-    ("T", "borrow", 1, 0),
     ("V", "copy b", 3, 0),
     ("S", "copy b", 3, 1),
-    ("S", "append", 1, 0),
-    ("D", "store", 1, 0),
-    ("V", "copy b", 3, 2),
+    ("V", "copy a", 3, 2),
+    ("S", "copy b", 3, 2),
     ("V", "quantise", 3, 0),
     ("S", "empty", 2, 0),
+    ("V", "quantise", 3, 1),
     ("S", "empty", 3, 0),
-    ("V", "quantise", 3, 2),
     ("T", "borrow", 2, 0),
-    ("T", "borrow", 3, 0),
     ("S", "append", 2, 0),
     ("D", "store", 2, 0),
+    ("V", "quantise", 3, 2),
     ("S", "append", 3, 0),
-    ("V", "quantise", 3, 1),
     ("V", "finish", 3, 0),
     ("D", "store", 3, 0),
 )
@@ -176,21 +180,31 @@ def tile_model_pa_s_kernel(tc, image, grad_output, grad_out, out):
                 in_=g_grouped[m][:, kh].rearrange("p kw c t -> p (kw c t)"),
             )
 
-        idle_bank = psum.tile([P, 8 * P], BF16)
+        regrouped = psum.tile([P, KW, P, PACK], BF16)
 
-        def heat(load, matmuls, transposes):
-            flat = g_raw[0][load][2][:].rearrange("p t c kh kw -> p (t c kh kw)")
-            for i in range(matmuls):
+        def regroup_on_tensor(load):
+            c0, width, part = g_raw[0][load]
+            for kw in range(KW):
                 nc.tensor.matmul(
-                    out=idle_bank[:, i * 2 * P : (i + 1) * 2 * P],
+                    out=regrouped[:, kw, c0 : c0 + width, :],
                     lhsT=ident[:],
-                    rhs=flat[:, i * 2 * P : (i + 1) * 2 * P],
+                    rhs=part[:, :, :, TENSOR_ROW, kw].rearrange("p t c -> p c t"),
                     start=True,
                     stop=True,
                 )
+
+        def fetch():
+            nc.scalar.copy(
+                out=g_grouped[0][:, TENSOR_ROW].rearrange("p kw c t -> p (kw c t)"),
+                in_=regrouped[:].rearrange("p kw c t -> p (kw c t)"),
+            )
+
+        def heat(transposes):
+            idle = psum.tile([P, 8 * P], BF16, name="extra1")
+            flat = g_raw[0][1][2][:].rearrange("p t c kh kw -> p (t c kh kw)")
             for i in range(transposes):
                 nc.tensor.transpose(
-                    idle_bank[:, (i % 8) * P : (i % 8 + 1) * P], flat[:, (i % 8) * P : (i % 8 + 1) * P], ident[:]
+                    idle[:, (i % 8) * P : (i % 8 + 1) * P], flat[:, (i % 8) * P : (i % 8 + 1) * P], ident[:]
                 )
 
         def multiply(m, kh):
@@ -198,6 +212,8 @@ def tile_model_pa_s_kernel(tc, image, grad_output, grad_out, out):
             last = KH_ORDER[m][-1]
             to = acc_rest if apart and kh > 0 else acc[m]
             for kw in range(KW):
+                if apart and kh == last and kw == KW - 1:
+                    borrow(m)
                 first_col = kw * KW_PITCH + (KH - 1 - kh) * BLOCK
                 window = slice(first_col, first_col + N_PASS)
                 nc.tensor.matmul_mx(
@@ -211,7 +227,7 @@ def tile_model_pa_s_kernel(tc, image, grad_output, grad_out, out):
                 )
 
         out_rows = out.rearrange("n (c k) r q -> c n (k r q)", k=4)
-        result, part, extra = [], [], []
+        result, extra = [], {}
 
         def row_view(bank, n):
             v = bank[:, 0 : ROWS * BLOCK].rearrange("p (b w) -> p b w", w=BLOCK)[:, :, 0 : W * SLOTS]
@@ -226,7 +242,7 @@ def tile_model_pa_s_kernel(tc, image, grad_output, grad_out, out):
                 )
 
         def borrow(m):
-            extra.append(psum.tile([P, N_PASS], F32, name="extra%d" % (m % 2)))
+            extra[m] = psum.tile([P, N_PASS], F32, name="extra%d" % (m % 2))
             nc.tensor.matmul(
                 out=extra[m][:, 0 : IMAGES * EXTRA],
                 lhsT=shift,
@@ -249,6 +265,11 @@ def tile_model_pa_s_kernel(tc, image, grad_output, grad_out, out):
                     in_=result[m][k:P:4, :, own : own + HEAD[k + 1] - HEAD[k]],
                 )
 
+        def store_rows(m):
+            nc.sync.dma_start(
+                out=out.rearrange("n c r q -> c n (r q)")[m * P : (m + 1) * P], in_=result[m][:, :, 0:GRID]
+            )
+
         def finish(m):
             for n in range(IMAGES):
                 v = result[m][:, n, 0:GRID].rearrange("p (f b q) -> p f b q", f=FOLDS, b=ROWS)
@@ -261,10 +282,12 @@ def tile_model_pa_s_kernel(tc, image, grad_output, grad_out, out):
                 regroup(nc.scalar.copy if engine == "S" else nc.vector.tensor_copy, m, kh, slice(0, 1))
             elif what == "copy b":
                 regroup(nc.scalar.copy if engine == "S" else nc.vector.tensor_copy, m, kh, slice(1, 2))
-            elif what == "heat a":
-                heat(0, m, kh)
-            elif what == "heat b":
-                heat(1, m, kh)
+            elif what == "regroup":
+                regroup_on_tensor(kh)
+            elif what == "heat":
+                heat(kh)
+            elif what == "fetch":
+                fetch()
             elif what == "quantise":
                 quantise(m, kh)
                 multiply(m, kh)
@@ -274,6 +297,8 @@ def tile_model_pa_s_kernel(tc, image, grad_output, grad_out, out):
                 borrow(m)
             elif what == "append":
                 append(m)
+            elif what == "store rows":
+                store_rows(m)
             elif what == "store":
                 store(m)
             else:

@@ -37,9 +37,9 @@ TENSOR_ROW = 2
 EXTRA = 6
 HEAD = (0, 96, 184, 272, 360)
 ORDER = (
+    ("T", "heat", 0, 0),
     ("T", "regroup", 0, 0),
     ("T", "regroup", 0, 1),
-    ("T", "heat", 0, 9),
     ("S", "copy a", 0, 0),
     ("S", "copy a", 0, 1),
     ("V", "copy b", 0, 0),
@@ -199,13 +199,10 @@ def tile_model_pa_s_kernel(tc, image, grad_output, grad_out, out):
                 in_=regrouped[:].rearrange("p kw c t -> p (kw c t)"),
             )
 
-        def heat(transposes):
-            idle = psum.tile([P, 8 * P], BF16, name="extra1")
-            flat = g_raw[0][1][2][:].rearrange("p t c kh kw -> p (t c kh kw)")
-            for i in range(transposes):
-                nc.tensor.transpose(
-                    idle[:, (i % 8) * P : (i % 8 + 1) * P], flat[:, (i % 8) * P : (i % 8 + 1) * P], ident[:]
-                )
+        def heat():
+            idle = psum.tile([P, N_PASS], F32, name="extra1")
+            words = y_raw[:].rearrange("p n t l -> p (n t l)").bitcast(F32)
+            nc.tensor.matmul(out=idle[:, 0:P], lhsT=wide[:, 0:P], rhs=words[:, 0:P], start=True, stop=True)
 
         def multiply(m, kh):
             apart = m == CI_TILES - 1
@@ -285,7 +282,7 @@ def tile_model_pa_s_kernel(tc, image, grad_output, grad_out, out):
             elif what == "regroup":
                 regroup_on_tensor(kh)
             elif what == "heat":
-                heat(kh)
+                heat()
             elif what == "fetch":
                 fetch()
             elif what == "quantise":

@@ -31,7 +31,7 @@ Y_COLS = (KW - 1) * KW_PITCH + (KH - 1) * BLOCK + N_PASS
 KW_STEP = KW_PITCH + SLOTS
 QUANT_BLOCKS = 8
 
-LOADS = (((0, 64), (64, 64)),) * CI_TILES
+HALVES = ((0, 64), (64, 64))
 KH_ORDER = ((0, 1, 2), (0, 1, 2), (0, 1, 2), (0, 1, 2))
 TENSOR_ROW = 2
 EXTRA = 6
@@ -115,11 +115,8 @@ def tile_model_pa_s_kernel(tc, image, grad_output, grad_out, out):
         g_rows = grad_out.rearrange("(p t) c kh kw -> p t c kh kw", t=PACK)
         g_raw = []
         for m in range(CI_TILES):
-            g_raw.append([])
-            for c0, width in LOADS[m]:
-                part = keep.tile([P, PACK, width, KH, KW], BF16, name="g_raw%d_%d" % (m, c0))
-                nc.sync.dma_start(out=part[:], in_=g_rows[:, :, m * P + c0 : m * P + c0 + width])
-                g_raw[m].append((c0, width, part))
+            g_raw.append(keep.tile([P, PACK, P, KH, KW], BF16, name="g_raw%d" % m))
+            nc.sync.dma_start(out=g_raw[m][:], in_=g_rows[:, :, m * P : (m + 1) * P])
 
         y_pad = keep.tile([P, QUANT_BLOCKS, WO, IMAGES, FOLDS, PACK], BF16, align_bytes=64)
         nc.vector.memset(y_pad[:], 0.0)
@@ -165,13 +162,11 @@ def tile_model_pa_s_kernel(tc, image, grad_output, grad_out, out):
             acc.append(psum.tile([P, N_PASS], F32, name="acc%d" % m))
         acc_rest = psum.tile([P, N_PASS], F32)
 
-        def regroup(engine_copy, m, kh, loads):
+        def regroup(engine_copy, m, kh, halves):
             g_to = g_grouped[m][:].rearrange("p kh kw c t -> p kh c t kw")
-            for c0, width, part in g_raw[m][loads]:
-                engine_copy(
-                    out=g_to[:, kh, c0 : c0 + width],
-                    in_=part[:].rearrange("p t c kh kw -> p kh c t kw")[:, kh],
-                )
+            g_from = g_raw[m][:].rearrange("p t c kh kw -> p kh c t kw")
+            for c0, width in HALVES[halves]:
+                engine_copy(out=g_to[:, kh, c0 : c0 + width], in_=g_from[:, kh, c0 : c0 + width])
 
         def quantise(m, kh):
             nc.vector.quantize_mx(
@@ -182,13 +177,13 @@ def tile_model_pa_s_kernel(tc, image, grad_output, grad_out, out):
 
         regrouped = psum.tile([P, KW, P, PACK], BF16)
 
-        def regroup_on_tensor(load):
-            c0, width, part = g_raw[0][load]
+        def regroup_on_tensor(half):
+            c0, width = HALVES[half]
             for kw in range(KW):
                 nc.tensor.matmul(
                     out=regrouped[:, kw, c0 : c0 + width, :],
                     lhsT=ident[:],
-                    rhs=part[:, :, :, TENSOR_ROW, kw].rearrange("p t c -> p c t"),
+                    rhs=g_raw[0][:, :, c0 : c0 + width, TENSOR_ROW, kw].rearrange("p t c -> p c t"),
                     start=True,
                     stop=True,
                 )

@@ -32,6 +32,7 @@ KW_STEP = KW_PITCH + SLOTS
 QUANT_BLOCKS = 8
 
 HALVES = ((0, 64), (64, 64))
+PARTS = {"copy": (0, P), "copy a": HALVES[0], "copy b": HALVES[1]}
 KH_ORDER = ((0, 1, 2), (0, 1, 2), (0, 1, 2), (0, 1, 2))
 TENSOR_ROW = 2
 EXTRA = 6
@@ -46,39 +47,33 @@ ORDER = (
     ("V", "copy b", 0, 1),
     ("S", "fetch", 0, 2),
     ("V", "quantise", 0, 0),
-    ("V", "copy a", 1, 0),
-    ("S", "copy a", 1, 1),
     ("V", "quantise", 0, 1),
-    ("V", "copy b", 1, 0),
-    ("S", "copy b", 1, 1),
+    ("V", "copy", 1, 0),
+    ("S", "copy", 1, 1),
     ("V", "quantise", 0, 2),
     ("V", "copy a", 1, 2),
     ("S", "copy b", 1, 2),
     ("V", "quantise", 1, 0),
     ("V", "quantise", 1, 1),
-    ("V", "copy a", 2, 0),
-    ("S", "copy a", 2, 1),
+    ("V", "copy", 2, 0),
+    ("S", "copy", 2, 1),
     ("V", "quantise", 1, 2),
-    ("V", "copy b", 2, 0),
-    ("S", "copy b", 2, 1),
-    ("S", "empty", 0, 0),
-    ("D", "store rows", 0, 0),
     ("V", "copy a", 2, 2),
     ("S", "copy b", 2, 2),
+    ("S", "empty", 0, 0),
+    ("D", "store rows", 0, 0),
     ("V", "quantise", 2, 0),
     ("V", "quantise", 2, 1),
-    ("V", "copy a", 3, 0),
-    ("S", "copy a", 3, 1),
-    ("S", "empty", 1, 0),
-    ("D", "store rows", 1, 0),
+    ("V", "copy", 3, 0),
+    ("S", "copy", 3, 1),
     ("V", "quantise", 2, 2),
-    ("V", "copy b", 3, 0),
-    ("S", "copy b", 3, 1),
+    ("V", "quantise", 3, 0),
     ("V", "copy a", 3, 2),
     ("S", "copy b", 3, 2),
-    ("V", "quantise", 3, 0),
-    ("S", "empty", 2, 0),
+    ("S", "empty", 1, 0),
+    ("D", "store rows", 1, 0),
     ("V", "quantise", 3, 1),
+    ("S", "empty", 2, 0),
     ("S", "empty", 3, 0),
     ("T", "borrow", 2, 0),
     ("S", "append", 2, 0),
@@ -162,17 +157,17 @@ def tile_model_pa_s_kernel(tc, image, grad_output, grad_out, out):
             acc.append(psum.tile([P, N_PASS], F32, name="acc%d" % m))
         acc_rest = psum.tile([P, N_PASS], F32)
 
-        def regroup(engine_copy, m, kh, halves):
+        def regroup(engine_copy, m, kh, what):
             g_to = g_grouped[m][:].rearrange("p kh kw c t -> p kh c t kw")
             g_from = g_raw[m][:].rearrange("p t c kh kw -> p kh c t kw")
-            for c0, width in HALVES[halves]:
-                engine_copy(out=g_to[:, kh, c0 : c0 + width], in_=g_from[:, kh, c0 : c0 + width])
+            c0, width = PARTS[what]
+            engine_copy(out=g_to[:, kh, c0 : c0 + width], in_=g_from[:, kh, c0 : c0 + width])
 
-        def quantise(m, kh):
+        def quantise(m, kh, taps):
             nc.vector.quantize_mx(
-                out=g_codes[m][:, kh].rearrange("p kw c -> p (kw c)").bitcast(E5M2_X4),
-                scales=g_scales[m][:, kh].rearrange("p kw c -> p (kw c)"),
-                in_=g_grouped[m][:, kh].rearrange("p kw c t -> p (kw c t)"),
+                out=g_codes[m][:, kh, taps].rearrange("p kw c -> p (kw c)").bitcast(E5M2_X4),
+                scales=g_scales[m][:, kh, taps].rearrange("p kw c -> p (kw c)"),
+                in_=g_grouped[m][:, kh, taps].rearrange("p kw c t -> p (kw c t)"),
             )
 
         regrouped = psum.tile([P, KW, P, PACK], BF16)
@@ -199,11 +194,11 @@ def tile_model_pa_s_kernel(tc, image, grad_output, grad_out, out):
             words = y_raw[:].rearrange("p n t l -> p (n t l)").bitcast(F32)
             nc.tensor.matmul(out=idle[:, 0:P], lhsT=wide[:, 0:P], rhs=words[:, 0:P], start=True, stop=True)
 
-        def multiply(m, kh):
+        def multiply(m, kh, taps):
             apart = m == CI_TILES - 1
             last = KH_ORDER[m][-1]
             to = acc_rest if apart and kh > 0 else acc[m]
-            for kw in range(KW):
+            for kw in range(KW)[taps]:
                 if apart and kh == last and kw == KW - 1:
                     borrow(m)
                 first_col = kw * KW_PITCH + (KH - 1 - kh) * BLOCK
@@ -221,17 +216,16 @@ def tile_model_pa_s_kernel(tc, image, grad_output, grad_out, out):
         out_rows = out.rearrange("n (c k) r q -> c n (k r q)", k=4)
         result, extra = [], {}
 
-        def row_view(bank, n):
+        def grid_of(bank):
             v = bank[:, 0 : ROWS * BLOCK].rearrange("p (b w) -> p b w", w=BLOCK)[:, :, 0 : W * SLOTS]
-            return v.rearrange("p b (q s) -> p s b q", s=SLOTS)[:, n * FOLDS : (n + 1) * FOLDS]
+            return v.rearrange("p b (q n f) -> p n f b q", n=IMAGES, f=FOLDS)
+
+        def rows_of(m):
+            return result[m][:, :, 0:GRID].rearrange("p n (f b q) -> p n f b q", f=FOLDS, b=ROWS)
 
         def empty(m):
             result.append(keep.tile([P, IMAGES, GRID + EXTRA], F32, name="result%d" % m))
-            for n in range(IMAGES):
-                nc.scalar.copy(
-                    out=result[m][:, n, 0:GRID].rearrange("p (f b q) -> p f b q", f=FOLDS, b=ROWS),
-                    in_=row_view(acc[m], n),
-                )
+            nc.scalar.copy(out=rows_of(m), in_=grid_of(acc[m]))
 
         def borrow(m):
             extra[m] = psum.tile([P, N_PASS], F32, name="extra%d" % (m % 2))
@@ -263,17 +257,11 @@ def tile_model_pa_s_kernel(tc, image, grad_output, grad_out, out):
             )
 
         def finish(m):
-            for n in range(IMAGES):
-                v = result[m][:, n, 0:GRID].rearrange("p (f b q) -> p f b q", f=FOLDS, b=ROWS)
-                nc.vector.tensor_add(out=v, in0=row_view(acc_rest, n), in1=v)
+            nc.vector.tensor_add(out=rows_of(m), in0=grid_of(acc_rest), in1=rows_of(m))
 
         for engine, what, m, kh in ORDER:
-            if what == "copy":
-                regroup(nc.scalar.copy if engine == "S" else nc.vector.tensor_copy, m, kh, slice(0, 2))
-            elif what == "copy a":
-                regroup(nc.scalar.copy if engine == "S" else nc.vector.tensor_copy, m, kh, slice(0, 1))
-            elif what == "copy b":
-                regroup(nc.scalar.copy if engine == "S" else nc.vector.tensor_copy, m, kh, slice(1, 2))
+            if what in PARTS:
+                regroup(nc.scalar.copy if engine == "S" else nc.vector.tensor_copy, m, kh, what)
             elif what == "regroup":
                 regroup_on_tensor(kh)
             elif what == "heat":
@@ -281,8 +269,9 @@ def tile_model_pa_s_kernel(tc, image, grad_output, grad_out, out):
             elif what == "fetch":
                 fetch()
             elif what == "quantise":
-                quantise(m, kh)
-                multiply(m, kh)
+                for taps in (slice(0, 1), slice(1, 2)) if (m, kh) == (CI_TILES - 1, KH - 1) else (slice(0, KW),):
+                    quantise(m, kh, taps)
+                    multiply(m, kh, taps)
             elif what == "empty":
                 empty(m)
             elif what == "borrow":

@@ -31,53 +31,47 @@ Y_COLS = (KW - 1) * KW_PITCH + (KH - 1) * BLOCK + N_PASS
 KW_STEP = KW_PITCH + SLOTS
 QUANT_BLOCKS = 8
 
-HALVES = ((0, 64), (64, 64))
-PARTS = {"copy": (0, P), "copy a": HALVES[0], "copy b": HALVES[1]}
+PARTS = {"copy": (0, P), "copy a": (0, 64), "copy b": (64, 64), "copy v": (0, 72), "copy s": (72, 56)}
 KH_ORDER = ((0, 1, 2), (0, 1, 2), (0, 1, 2), (0, 1, 2))
-TENSOR_ROW = 2
 EXTRA = 6
 HEAD = (0, 96, 184, 272, 360)
 ORDER = (
     ("T", "heat", 0, 0),
-    ("T", "regroup", 0, 0),
-    ("T", "regroup", 0, 1),
     ("S", "copy a", 0, 0),
-    ("S", "copy a", 0, 1),
     ("V", "copy b", 0, 0),
-    ("V", "copy b", 0, 1),
-    ("S", "fetch", 0, 2),
+    ("S", "copy", 0, 2),
+    ("V", "copy a", 0, 1),
     ("V", "quantise", 0, 0),
+    ("V", "copy b", 0, 1),
     ("V", "quantise", 0, 1),
     ("V", "copy", 1, 0),
     ("S", "copy", 1, 1),
     ("V", "quantise", 0, 2),
-    ("V", "copy a", 1, 2),
-    ("S", "copy b", 1, 2),
+    ("V", "copy v", 1, 2),
+    ("S", "copy s", 1, 2),
     ("V", "quantise", 1, 0),
     ("V", "quantise", 1, 1),
     ("V", "copy", 2, 0),
     ("S", "copy", 2, 1),
     ("V", "quantise", 1, 2),
-    ("V", "copy a", 2, 2),
-    ("S", "copy b", 2, 2),
     ("S", "empty", 0, 0),
     ("D", "store rows", 0, 0),
+    ("V", "copy v", 2, 2),
+    ("S", "copy s", 2, 2),
     ("V", "quantise", 2, 0),
     ("V", "quantise", 2, 1),
     ("V", "copy", 3, 0),
     ("S", "copy", 3, 1),
     ("V", "quantise", 2, 2),
     ("V", "quantise", 3, 0),
-    ("V", "copy a", 3, 2),
-    ("S", "copy b", 3, 2),
+    ("V", "copy v", 3, 2),
+    ("S", "copy s", 3, 2),
     ("S", "empty", 1, 0),
     ("D", "store rows", 1, 0),
-    ("V", "quantise", 3, 1),
     ("S", "empty", 2, 0),
+    ("D", "store rows", 2, 0),
+    ("V", "quantise", 3, 1),
     ("S", "empty", 3, 0),
-    ("T", "borrow", 2, 0),
-    ("S", "append", 2, 0),
-    ("D", "store", 2, 0),
     ("V", "quantise", 3, 2),
     ("S", "append", 3, 0),
     ("V", "finish", 3, 0),
@@ -102,8 +96,6 @@ def tile_model_pa_s_kernel(tc, image, grad_output, grad_out, out):
         make_identity(nc, wide[:, 0:P])
         nc.gpsimd.memset(wide[:, P : P + 1], 0.0)
         shift = wide[:, 1 : P + 1]
-        ident = keep.tile([P, P], BF16)
-        nc.vector.tensor_copy(out=ident[:], in_=wide[:, 0:P])
 
         y_raw = keep.tile([P, IMAGES, PACK, HO * WO], BF16)
         nc.sync.dma_start(out=y_raw[:], in_=grad_output.rearrange("n (p t) i j -> p n t (i j)", t=PACK))
@@ -170,29 +162,13 @@ def tile_model_pa_s_kernel(tc, image, grad_output, grad_out, out):
                 in_=g_grouped[m][:, kh, taps].rearrange("p kw c t -> p (kw c t)"),
             )
 
-        regrouped = psum.tile([P, KW, P, PACK], BF16)
-
-        def regroup_on_tensor(half):
-            c0, width = HALVES[half]
-            for kw in range(KW):
-                nc.tensor.matmul(
-                    out=regrouped[:, kw, c0 : c0 + width, :],
-                    lhsT=ident[:],
-                    rhs=g_raw[0][:, :, c0 : c0 + width, TENSOR_ROW, kw].rearrange("p t c -> p c t"),
-                    start=True,
-                    stop=True,
-                )
-
-        def fetch():
-            nc.scalar.copy(
-                out=g_grouped[0][:, TENSOR_ROW].rearrange("p kw c t -> p (kw c t)"),
-                in_=regrouped[:].rearrange("p kw c t -> p (kw c t)"),
-            )
-
         def heat():
-            idle = psum.tile([P, N_PASS], F32, name="extra1")
+            idle = psum.tile([P, N_PASS], F32, name="extra")
             words = y_raw[:].rearrange("p n t l -> p (n t l)").bitcast(F32)
-            nc.tensor.matmul(out=idle[:, 0:P], lhsT=wide[:, 0:P], rhs=words[:, 0:P], start=True, stop=True)
+            for width in (256, 256, 64):
+                nc.tensor.matmul(
+                    out=idle[:, 0:width], lhsT=wide[:, 0:P], rhs=words[:, 0:width], start=True, stop=True
+                )
 
         def multiply(m, kh, taps):
             apart = m == CI_TILES - 1
@@ -228,7 +204,7 @@ def tile_model_pa_s_kernel(tc, image, grad_output, grad_out, out):
             nc.scalar.copy(out=rows_of(m), in_=grid_of(acc[m]))
 
         def borrow(m):
-            extra[m] = psum.tile([P, N_PASS], F32, name="extra%d" % (m % 2))
+            extra[m] = psum.tile([P, N_PASS], F32, name="extra")
             nc.tensor.matmul(
                 out=extra[m][:, 0 : IMAGES * EXTRA],
                 lhsT=shift,
@@ -262,20 +238,14 @@ def tile_model_pa_s_kernel(tc, image, grad_output, grad_out, out):
         for engine, what, m, kh in ORDER:
             if what in PARTS:
                 regroup(nc.scalar.copy if engine == "S" else nc.vector.tensor_copy, m, kh, what)
-            elif what == "regroup":
-                regroup_on_tensor(kh)
             elif what == "heat":
                 heat()
-            elif what == "fetch":
-                fetch()
             elif what == "quantise":
                 for taps in (slice(0, 1), slice(1, 2)) if (m, kh) == (CI_TILES - 1, KH - 1) else (slice(0, KW),):
                     quantise(m, kh, taps)
                     multiply(m, kh, taps)
             elif what == "empty":
                 empty(m)
-            elif what == "borrow":
-                borrow(m)
             elif what == "append":
                 append(m)
             elif what == "store rows":

@@ -150,10 +150,10 @@ def tile_model_pa_s_kernel(tc, image, grad_output, grad_out, out):
         acc_rest = psum.tile([P, N_PASS], F32)
 
         def regroup(engine_copy, m, kh, what):
-            g_to = g_grouped[m][:].rearrange("p kh kw c t -> p kh c t kw")
-            g_from = g_raw[m][:].rearrange("p t c kh kw -> p kh c t kw")
             c0, width = PARTS[what]
-            engine_copy(out=g_to[:, kh, c0 : c0 + width], in_=g_from[:, kh, c0 : c0 + width])
+            g_to = g_grouped[m][:, kh, :, c0 : c0 + width].rearrange("p kw (cb ci) t -> p cb t ci kw", ci=2)
+            g_from = g_raw[m][:, :, c0 : c0 + width, kh].rearrange("p t (cb ci) kw -> p cb t ci kw", ci=2)
+            engine_copy(out=g_to, in_=g_from)
 
         def quantise(m, kh, taps):
             nc.vector.quantize_mx(

from contextlib import ExitStack

import concourse.mybir as mybir
from concourse.masks import make_identity

BF16 = mybir.dt.bfloat16
F32 = mybir.dt.float32
I32 = mybir.dt.int32
U32 = mybir.dt.uint32
U8 = mybir.dt.uint8
E4M3_X4 = mybir.dt.float8_e4m3fn_x4
E5M2_X4 = mybir.dt.float8_e5m2_x4

P = 128
PACK = 4
IMAGES, CI, CO = 2, 512, 512
H, W = 10, 9
KH, KW = 3, 2
HO, WO = H - KH + 1, W - KW + 1
TAPS = KH * KW
CI_TILES = CI // P
N_PASS = 512
FOLDS = 2
ROWS = H // FOLDS
GRID = H * W
BLOCK = 64
SLOTS = IMAGES * FOLDS
BUF_BLOCKS = ROWS + KH - 1
KW_PITCH = BUF_BLOCKS * BLOCK
Y_COLS = (KW - 1) * KW_PITCH + (KH - 1) * BLOCK + N_PASS
KW_STEP = KW_PITCH + SLOTS
QUANT_BLOCKS = 8

PARTS = {"copy": (0, P), "copy a": (0, 64), "copy b": (64, 64), "copy v": (0, 72), "copy s": (72, 56)}
KH_ORDER = ((0, 1, 2), (0, 1, 2), (0, 1, 2), (0, 1, 2))
EXTRA = 6
HEAD = (0, 96, 184, 272, 360)
ORDER = (
    ("T", "heat", 0, 0),
    ("S", "copy a", 0, 0),
    ("V", "copy b", 0, 0),
    ("S", "copy", 0, 2),
    ("V", "copy a", 0, 1),
    ("V", "quantise", 0, 0),
    ("V", "copy b", 0, 1),
    ("V", "quantise", 0, 1),
    ("V", "copy", 1, 0),
    ("S", "copy", 1, 1),
    ("V", "quantise", 0, 2),
    ("V", "copy v", 1, 2),
    ("S", "copy s", 1, 2),
    ("V", "quantise", 1, 0),
    ("V", "quantise", 1, 1),
    ("V", "copy", 2, 0),
    ("S", "copy", 2, 1),
    ("V", "quantise", 1, 2),
    ("S", "empty", 0, 0),
    ("D", "store rows", 0, 0),
    ("V", "copy v", 2, 2),
    ("S", "copy s", 2, 2),
    ("V", "quantise", 2, 0),
    ("V", "quantise", 2, 1),
    ("V", "copy", 3, 0),
    ("S", "copy", 3, 1),
    ("V", "quantise", 2, 2),
    ("V", "quantise", 3, 0),
    ("V", "copy v", 3, 2),
    ("S", "copy s", 3, 2),
    ("S", "empty", 1, 0),
    ("D", "store rows", 1, 0),
    ("S", "empty", 2, 0),
    ("D", "store rows", 2, 0),
    ("V", "quantise", 3, 1),
    ("S", "empty", 3, 0),
    ("V", "quantise", 3, 2),
    ("S", "append", 3, 0),
    ("V", "finish", 3, 0),
    ("D", "store", 3, 0),
)

FLOPS = 2 * CO * CI * TAPS * IMAGES * HO * WO
BYTES = 2 * IMAGES * CO * HO * WO + 2 * CO * CI * TAPS + 4 * IMAGES * CI * H * W


def tile_model_pa_s_kernel(tc, image, grad_output, grad_out, out):
    nc = tc.nc
    with ExitStack() as ctx:
        keep = ctx.enter_context(tc.tile_pool(name="keep", bufs=1))
        psum = ctx.enter_context(tc.psum_pool(name="psum", bufs=1))
        ctx.enter_context(tc.manual_schedule())

        warm = keep.tile([P, 2], F32)
        nc.gpsimd.memset(warm[:, 0:1], 0.0)
        nc.scalar.copy(out=warm[:, 1:2], in_=warm[:, 0:1])
        wide = keep.tile([P, P + 1], F32)
        make_identity(nc, wide[:, 0:P])
        nc.gpsimd.memset(wide[:, P : P + 1], 0.0)
        shift = wide[:, 1 : P + 1]

        y_raw = keep.tile([P, IMAGES, PACK, HO * WO], BF16)
        nc.sync.dma_start(out=y_raw[:], in_=grad_output.rearrange("n (p t) i j -> p n t (i j)", t=PACK))
        g_rows = grad_out.rearrange("(p t) c kh kw -> p t c kh kw", t=PACK)
        g_raw = []
        for m in range(CI_TILES):
            g_raw.append(keep.tile([P, PACK, P, KH, KW], BF16, name="g_raw%d" % m))
            nc.sync.dma_start(out=g_raw[m][:], in_=g_rows[:, :, m * P : (m + 1) * P])

        y_pad = keep.tile([P, QUANT_BLOCKS, WO, IMAGES, FOLDS, PACK], BF16, align_bytes=64)
        nc.vector.memset(y_pad[:], 0.0)
        y_codes = keep.tile([P, Y_COLS], I32, align_bytes=64)
        y_scales = keep.tile([P, Y_COLS], U8, align_bytes=64)
        nc.vector.memset(y_scales[:].bitcast(I32), 0)
        nc.gpsimd.memset(y_codes[:].bitcast(F32), 0.0)
        for fold, engine_copy in ((0, nc.vector.tensor_copy), (1, nc.scalar.copy)):
            i0 = fold * (HO - ROWS)
            g0 = i0 - ROWS * fold + KH - 1
            engine_copy(
                out=y_pad[:, g0 : g0 + ROWS, :, :, fold, :].rearrange("p g j n t -> p (g j) n t"),
                in_=y_raw[:, :, :, i0 * WO : (i0 + ROWS) * WO].rearrange("p n t l -> p l n t"),
            )
        y_quant_cols = QUANT_BLOCKS * WO * SLOTS
        yq_codes = keep.tile([P, y_quant_cols], I32, align_bytes=64)
        yq_scales = keep.tile([P, y_quant_cols], U8, align_bytes=64)
        nc.vector.quantize_mx(
            out=yq_codes[:].bitcast(E4M3_X4),
            scales=yq_scales[:],
            in_=y_pad[:].rearrange("p g j n f t -> p (g j n f t)"),
        )

        def buffers(flat, unit):
            v = flat[:, 0 : KW * KW_STEP // unit].rearrange("p (kw a) -> p kw a", kw=KW)
            v = v[:, :, 0 : KW_PITCH // unit].rearrange("p kw (g w) -> p kw g w", g=BUF_BLOCKS)
            return v[:, :, :, 0 : WO * SLOTS // unit]

        def repeated(flat, unit):
            v = flat[:, 0 : BUF_BLOCKS * WO * SLOTS // unit].rearrange("p (g w) -> p g w", g=BUF_BLOCKS)
            return v.unsqueeze(1).to_broadcast([P, KW, BUF_BLOCKS, WO * SLOTS // unit])

        nc.vector.tensor_copy(out=buffers(y_codes[:], 1), in_=repeated(yq_codes[:], 1))
        nc.vector.tensor_copy(
            out=buffers(y_scales[:].bitcast(I32), 4), in_=repeated(yq_scales[:].bitcast(I32), 4)
        )

        g_grouped, g_codes, g_scales, acc = [], [], [], []
        for m in range(CI_TILES):
            g_grouped.append(keep.tile([P, KH, KW, P, PACK], BF16, align_bytes=64, name="g_grouped%d" % m))
            g_codes.append(keep.tile([P, KH, KW, P], U32, align_bytes=64, name="g_codes%d" % m))
            g_scales.append(keep.tile([P, KH, KW, P], U8, align_bytes=64, name="g_scales%d" % m))
            acc.append(psum.tile([P, N_PASS], F32, name="acc%d" % m))
        acc_rest = psum.tile([P, N_PASS], F32)

        def regroup(engine_copy, m, kh, what):
            c0, width = PARTS[what]
            g_to = g_grouped[m][:, kh, :, c0 : c0 + width].rearrange("p kw (cb ci) t -> p cb t ci kw", ci=2)
            g_from = g_raw[m][:, :, c0 : c0 + width, kh].rearrange("p t (cb ci) kw -> p cb t ci kw", ci=2)
            engine_copy(out=g_to, in_=g_from)

        def quantise(m, kh, taps):
            nc.vector.quantize_mx(
                out=g_codes[m][:, kh, taps].rearrange("p kw c -> p (kw c)").bitcast(E5M2_X4),
                scales=g_scales[m][:, kh, taps].rearrange("p kw c -> p (kw c)"),
                in_=g_grouped[m][:, kh, taps].rearrange("p kw c t -> p (kw c t)"),
            )

        def heat():
            idle = psum.tile([P, N_PASS], F32, name="extra")
            words = y_raw[:].rearrange("p n t l -> p (n t l)").bitcast(F32)
            for width in (256, 256, 64):
                nc.tensor.matmul(
                    out=idle[:, 0:width], lhsT=wide[:, 0:P], rhs=words[:, 0:width], start=True, stop=True
                )

        def multiply(m, kh, taps):
            apart = m == CI_TILES - 1
            last = KH_ORDER[m][-1]
            to = acc_rest if apart and kh > 0 else acc[m]
            for kw in range(KW)[taps]:
                if apart and kh == last and kw == KW - 1:
                    borrow(m)
                first_col = kw * KW_PITCH + (KH - 1 - kh) * BLOCK
                window = slice(first_col, first_col + N_PASS)
                nc.tensor.matmul_mx(
                    out=to[:],
                    lhsT=g_codes[m][:, kh, kw, :].bitcast(E5M2_X4),
                    lhsT_scale=g_scales[m][:, kh, kw, :],
                    rhs=y_codes[:, window].bitcast(E4M3_X4),
                    rhs_scale=y_scales[:, window],
                    start=(kw == 0 and kh in (KH_ORDER[m][0], KH_ORDER[m][1] if apart else KH_ORDER[m][0])),
                    stop=(kw == KW - 1 and kh in (last, KH_ORDER[m][0] if apart else last)),
                )

        out_rows = out.rearrange("n (c k) r q -> c n (k r q)", k=4)
        result, extra = [], {}

        def grid_of(bank):
            v = bank[:, 0 : ROWS * BLOCK].rearrange("p (b w) -> p b w", w=BLOCK)[:, :, 0 : W * SLOTS]
            return v.rearrange("p b (q n f) -> p n f b q", n=IMAGES, f=FOLDS)

        def rows_of(m):
            return result[m][:, :, 0:GRID].rearrange("p n (f b q) -> p n f b q", f=FOLDS, b=ROWS)

        def empty(m):
            result.append(keep.tile([P, IMAGES, GRID + EXTRA], F32, name="result%d" % m))
            nc.scalar.copy(out=rows_of(m), in_=grid_of(acc[m]))

        def borrow(m):
            extra[m] = psum.tile([P, N_PASS], F32, name="extra")
            nc.tensor.matmul(
                out=extra[m][:, 0 : IMAGES * EXTRA],
                lhsT=shift,
                rhs=result[m][:, :, 0:EXTRA],
                start=True,
                stop=True,
            )

        def append(m):
            nc.scalar.copy(
                out=result[m][:, :, GRID : GRID + EXTRA],
                in_=extra[m][:, 0 : IMAGES * EXTRA].rearrange("p (n e) -> p n e", n=IMAGES),
            )

        def store(m):
            for k in range(4):
                own = HEAD[k] - k * GRID
                nc.sync.dma_start(
                    out=out_rows[m * P // 4 : (m + 1) * P // 4, :, HEAD[k] : HEAD[k + 1]],
                    in_=result[m][k:P:4, :, own : own + HEAD[k + 1] - HEAD[k]],
                )

        def store_rows(m):
            nc.sync.dma_start(
                out=out.rearrange("n c r q -> c n (r q)")[m * P : (m + 1) * P], in_=result[m][:, :, 0:GRID]
            )

        def finish(m):
            nc.vector.tensor_add(out=rows_of(m), in0=grid_of(acc_rest), in1=rows_of(m))

        for engine, what, m, kh in ORDER:
            if what in PARTS:
                regroup(nc.scalar.copy if engine == "S" else nc.vector.tensor_copy, m, kh, what)
            elif what == "heat":
                heat()
            elif what == "quantise":
                for taps in (slice(0, 1), slice(1, 2)) if (m, kh) == (CI_TILES - 1, KH - 1) else (slice(0, KW),):
                    quantise(m, kh, taps)
                    multiply(m, kh, taps)
            elif what == "empty":
                empty(m)
            elif what == "append":
                append(m)
            elif what == "store rows":
                store_rows(m)
            elif what == "store":
                store(m)
            else:
                finish(m)
